import numpy as np
import ml_dtypes


def mxq(x, axis, fmt="e4m3"):
    dtype, down = {"e4m3": (ml_dtypes.float8_e4m3fn, 7), "e5m2": (ml_dtypes.float8_e5m2, 14)}[fmt]
    v = np.moveaxis(np.asarray(x, np.float32).astype(ml_dtypes.bfloat16).astype(np.float64), axis, -1)
    blocks = v.reshape(v.shape[:-1] + (-1, 32))
    amax = np.abs(blocks).max(-1, keepdims=True)
    byte = np.maximum(np.where(amax > 0, np.frexp(amax)[1] - 1 + 127, 0) - down, 1)
    scale = np.exp2(byte - 127.0)
    codes = (blocks / scale).astype(np.float32).astype(dtype).astype(np.float64)
    return np.moveaxis((codes * scale).reshape(v.shape), -1, axis)


WIDE = False


def mx_kscale(k):
    if not WIDE:
        return np.ones(k)
    levels = np.array([10, -10, 5, -5, 0])
    a = np.random.permutation(np.resize(levels, k // 512 * 4)).reshape(k // 512, 4)
    idx = np.arange(k)
    return np.exp2(a[idx // 512, idx % 128 // 32])


BF16 = ml_dtypes.bfloat16


def bf(x):
    return np.asarray(x, np.float32).astype(BF16)


def f64(x):
    return np.asarray(x).astype(np.float64)


E2M1 = np.array([0.0, 0.5, 1.0, 1.5, 2.0, 3.0, 4.0, 6.0, -0.0, -0.5, -1.0, -1.5, -2.0, -3.0, -4.0, -6.0])


def pack_weight(w, fmt):
    k, n = w.shape
    w = f64(bf(w)).reshape(k // 32, 32, n)
    amax = np.abs(w).max(1)
    if fmt == "e4m3":
        byte = np.frexp(amax)[1] - 1 + 127 - 7
    else:
        mant, ex = np.frexp(amax / 6.0)
        byte = np.where(mant > 0.5, ex, ex - 1) + 127
    byte = np.clip(np.where(amax > 0, byte, 1), 1, 254)
    scaled = (w * np.exp2(127.0 - byte)[:, None, :]).reshape(k, n).astype(np.float32)
    by_word = np.ascontiguousarray(scaled.reshape(k // 512, 128, 4, n).transpose(0, 1, 3, 2))
    if fmt == "e4m3":
        words = by_word.astype(ml_dtypes.float8_e4m3fn).view(np.uint8)
    else:
        c = by_word.astype(ml_dtypes.float4_e2m1fn).view(np.uint8) & 0xF
        words = c[..., 0::2] | (c[..., 1::2] << 4)
    return np.ascontiguousarray(words), np.ascontiguousarray(byte.astype(np.uint8).reshape(k // 512, 16, n))


def unpack_weight(words, scales, fmt):
    g, p, n, _ = words.shape
    if fmt == "e4m3":
        vals = np.ascontiguousarray(words).view(ml_dtypes.float8_e4m3fn).astype(np.float64)
    else:
        nib = np.empty((g, p, n, 4), np.uint8)
        nib[..., 0::2] = words & 0xF
        nib[..., 1::2] = words >> 4
        vals = E2M1[nib]
    vals = vals * np.repeat(np.exp2(scales.astype(np.float64) - 127.0), 8, axis=1)[..., None]
    return vals.transpose(0, 1, 3, 2).reshape(g * 512, n)

def pack4(w):
    words, scales = pack_weight(w, "e2m1")
    return words.reshape(words.shape[0], 128, -1), scales


def unpack4(words, scales):
    return unpack_weight(words.reshape(words.shape[0], 128, -1, 2), scales, "e2m1")


B, D, M, C = 256, 2048, 8, 512


def setup_inputs():
    s = mx_kscale(D)
    scale = 1.0 / np.sqrt(D)
    x = bf(np.random.standard_normal((B, D)) * s)
    model_weights = bf(np.random.standard_normal((M, D, C)) * scale / s[None, :, None])
    model_bias = bf(np.random.standard_normal((M, C)) * 0.1)
    rw_words, rw_scales = pack4(np.random.standard_normal((D, M * C)) * scale / s[:, None])
    resnet_bias = bf(np.random.standard_normal(M * C) * 0.1)
    return {
        "x": x,
        "model_weights": model_weights,
        "model_bias": model_bias,
        "resnet_weight_words": rw_words,
        "resnet_weight_scales": rw_scales,
        "resnet_bias": resnet_bias,
    }


def reference(x, model_weights, model_bias, resnet_weight_words, resnet_weight_scales, resnet_bias):
    xq = mxq(f64(x), 1, "e4m3")
    mw = mxq(f64(model_weights), 1, "e4m3")
    rw = unpack4(resnet_weight_words, resnet_weight_scales)
    outputs = np.einsum("bd,mdc->bmc", xq, mw, optimize=True) + f64(model_bias)[None, :, :]
    w = ((xq @ rw) + f64(resnet_bias)).reshape(x.shape[0], model_weights.shape[0], model_weights.shape[2])
    return np.sum(outputs * w, axis=1)

@@ -1,0 +1,295 @@
+from contextlib import ExitStack
+
+import concourse.bass as bass
+import concourse.mybir as mybir
+import concourse.tile as tile
+from concourse.masks import make_identity
+
+FP8X4 = mybir.dt.float8_e4m3fn_x4
+FP4X4 = mybir.dt.float4_e2m1fn_x4
+BF16 = mybir.dt.bfloat16
+F32 = mybir.dt.float32
+I32 = mybir.dt.int32
+U32 = mybir.dt.uint32
+U8 = mybir.dt.uint8
+ACT = mybir.ActivationFunctionType
+ALU = mybir.AluOpType
+
+B, D, M, C = 256, 2048, 8, 512
+P = 128
+G = D // 512
+CT = C // P
+BT = B // P
+FLOPS = 2 * 2 * B * D * M * C
+
+MANUAL = True
+GROUPS = [1] * 8
+RAW_BUFS = 12
+
+
+def tile_multi_fuse_pic_cls_kernel(
+    tc, x, model_weights, model_bias, resnet_weight_words, resnet_weight_scales, resnet_bias, out
+):
+    nc = tc.nc
+    with ExitStack() as ctx:
+        sb = ctx.enter_context(tc.tile_pool(name="sb", bufs=1))
+        ps = ctx.enter_context(tc.psum_pool(name="ps", bufs=1))
+        if MANUAL:
+            ctx.enter_context(tc.manual_schedule())
+
+        rs = sb.tile([P, G, M * C], U8, name="rs", align_bytes=64)
+        for mp in range(4):
+            nc.vector.memset(rs[:, :, 1024 * mp : 1024 * (mp + 1)].bitcast(I32), 0)
+        bias_rows = sb.tile([P, P], BF16, name="bias_rows")
+        nc.vector.memset(bias_rows[:], 0.0)
+        ident_f = sb.tile([P, P], F32, name="ident_f")
+        make_identity(nc, ident_f[:])
+        ident_b = sb.tile([P, P], BF16, name="ident_b")
+        make_identity(nc, ident_b[:])
+
+        nc.scalar.dma_start(out=bias_rows[0:32, :], in_=model_bias.rearrange("m (t c) -> (m t) c", c=P))
+        nc.scalar.dma_start(out=bias_rows[32:64, :], in_=resnet_bias.rearrange("(r c) -> r c", c=P))
+
+        raw = {}
+        x_sb = []
+        rwt = []
+
+        def load_mw(m, g):
+            t = sb.tile([P, 4, C], BF16, name="raw_%d_%d" % (m, g), tag="raw", bufs=RAW_BUFS)
+            nc.sync.dma_start(
+                out=t[:], in_=model_weights[m, 512 * g : 512 * (g + 1), :].rearrange("(p j) c -> p j c", j=4)
+            )
+            raw[(m, g)] = t
+
+        def load_x(bt):
+            t = sb.tile([P, D], BF16, name="x_sb_%d" % bt)
+            nc.sync.dma_start(out=t[:], in_=x[P * bt : P * (bt + 1), :])
+            x_sb.append(t)
+
+        scales_qgn = resnet_weight_scales.rearrange("g q n -> q g n")
+        words_pgn = resnet_weight_words.rearrange("g p n -> p g n")
+
+        def load_rw(mp):
+            n0 = 1024 * mp
+            for b in range(2):
+                for r in range(4):
+                    nc.sync.dma_start(
+                        out=rs[32 * b + r : P : 64, :, n0 : n0 + 1024].bitcast(I32),
+                        in_=scales_qgn[4 * b + r : 16 : 8, :, n0 : n0 + 1024].bitcast(I32),
+                    )
+            t = sb.tile([P, G, 2048], U8, name="rwt_%d" % mp, align_bytes=64)
+            nc.sync.dma_start(out=t[:].bitcast(I32), in_=words_pgn[:, :, 2048 * mp : 2048 * (mp + 1)].bitcast(I32))
+            rwt.append(t)
+
+        load_mw(0, 0)
+        load_x(0)
+        load_x(1)
+        for g in range(1, G):
+            load_mw(0, g)
+        load_rw(0)
+        for g in range(G):
+            load_mw(1, g)
+        for mp in range(1, 4):
+            load_rw(mp)
+            for m in (2 * mp, 2 * mp + 1):
+                for g in range(G):
+                    load_mw(m, g)
+
+        grp = {}
+        cod = {}
+        sca = {}
+
+        def rg(m, g):
+            t = sb.tile([P, C, 4], BF16, name="grp_%d_%d" % (m, g), tag="grp", bufs=4, align_bytes=64)
+            dst = t[:].rearrange("p (c i) t -> p c t i", i=4)
+            src = raw[(m, g)][:].rearrange("p t (c i) -> p c t i", i=4)
+            if g % 2 == 0:
+                nc.vector.tensor_copy(out=dst, in_=src)
+            else:
+                nc.scalar.copy(out=dst, in_=src)
+            grp[(m, g)] = t
+
+        def q(m, g):
+            if g == 0:
+                cod[m] = sb.tile([P, G, C], U32, name="cod_%d" % m, tag="cod", bufs=3, align_bytes=64)
+                sca[m] = sb.tile([P, G, C], U8, name="sca_%d" % m, tag="sca", bufs=3, align_bytes=64)
+            nc.vector.quantize_mx(
+                out=cod[m][:, g, :].bitcast(FP8X4),
+                scales=sca[m][:, g, :],
+                in_=grp[(m, g)][:].rearrange("p c t -> p (c t)"),
+            )
+
+        xq = sb.tile([P, G, B], U32, name="xq", align_bytes=64)
+        xs = sb.tile([P, G, B], U8, name="xs", align_bytes=64)
+        o_ps = {}
+        w_ps = {}
+        w_sb = {}
+
+        def o_pass(m, h):
+            t = ps.tile([P, 2, B], F32, name="o_%d_%d" % (m, h), tag="o", bufs=3)
+            for ctl in range(2):
+                c0 = P * (2 * h + ctl)
+                for g in range(G):
+                    nc.tensor.matmul_mx(
+                        out=t[:, ctl, :],
+                        lhsT=cod[m][:, g, c0 : c0 + P].bitcast(FP8X4),
+                        lhsT_scale=sca[m][:, g, c0 : c0 + P],
+                        rhs=xq[:, g, :].bitcast(FP8X4),
+                        rhs_scale=xs[:, g, :],
+                        start=(g == 0),
+                        stop=(g == G - 1),
+                    )
+            o_ps[(m, h)] = t
+
+        def w_pass(m, h):
+            t = ps.tile([P, 2, B], F32, name="w_%d_%d" % (m, h), tag="w", bufs=3)
+            for ctl in range(2):
+                ct = 2 * h + ctl
+                n0 = C * m + P * ct
+                w0 = 2 * (C * (m % 2) + P * ct)
+                for bt in range(BT):
+                    for g in range(G):
+                        nc.tensor.matmul_mx(
+                            out=t[:, ctl, P * bt : P * (bt + 1)],
+                            lhsT=rwt[m // 2][:, g, w0 : w0 + 2 * P].bitcast(FP4X4),
+                            lhsT_scale=rs[:, g, n0 : n0 + P],
+                            rhs=xq[:, g, P * bt : P * (bt + 1)].bitcast(FP8X4),
+                            rhs_scale=xs[:, g, P * bt : P * (bt + 1)],
+                            start=(g == 0),
+                            stop=(g == G - 1),
+                        )
+            w_ps[(m, h)] = t
+
+        bias_t = sb.tile([P, 64], F32, name="bias_t")
+
+        def evac(m, h):
+            t = sb.tile([P, 2, B], F32, name="wsb_%d_%d" % (m, h), tag="wsb", bufs=6)
+            for ctl in range(2):
+                col = 32 + CT * m + 2 * h + ctl
+                nc.scalar.activation(
+                    out=t[:, ctl, :], in_=w_ps[(m, h)][:, ctl, :], func=ACT.Identity,
+                    bias=bias_t[:, col : col + 1], scale=1.0,
+                )
+            w_sb[(m, h)] = t
+
+        group_of = {}
+        first_of = {}
+        last_of = {}
+        m0 = 0
+        for gi, size in enumerate(GROUPS):
+            for m in range(m0, m0 + size):
+                group_of[m] = gi
+                first_of[m] = m == m0
+                last_of[m] = m == m0 + size - 1
+            m0 += size
+        s_sb = {}
+
+        def stt(m, h):
+            gi = group_of[m]
+            if first_of[m]:
+                s_sb[(gi, h)] = sb.tile([P, 2, B], F32, name="s_%d_%d" % (gi, h), tag="s", bufs=6)
+                dst = s_sb[(gi, h)]
+            else:
+                dst = sb.tile([P, 2, B], F32, name="p_%d_%d" % (m, h), tag="p", bufs=3)
+            for ctl in range(2):
+                col = CT * m + 2 * h + ctl
+                nc.vector.scalar_tensor_tensor(
+                    out=dst[:, ctl, :], in0=o_ps[(m, h)][:, ctl, :], scalar=bias_t[:, col : col + 1],
+                    in1=w_sb[(m, h)][:, ctl, :], op0=ALU.add, op1=ALU.mult,
+                )
+            if not first_of[m]:
+                nc.vector.tensor_tensor(out=s_sb[(gi, h)][:], in0=s_sb[(gi, h)][:], in1=dst[:], op=ALU.add)
+
+        acc = [ps.tile([P, C], F32, name="acc_%d" % bt) for bt in range(BT)]
+
+        def acc_t(gi):
+            for h in range(2):
+                for ctl in range(2):
+                    c0 = P * (2 * h + ctl)
+                    for bt in range(BT):
+                        nc.tensor.matmul(
+                            out=acc[bt][:, c0 : c0 + P],
+                            lhsT=s_sb[(gi, h)][:, ctl, P * bt : P * (bt + 1)],
+                            rhs=ident_f[:],
+                            start=(gi == 0 and h == 0 and ctl == 0),
+                            stop=(gi == len(GROUPS) - 1 and h == 1 and ctl == 1),
+                            is_transpose=True,
+                        )
+
+        rg(0, 0)
+        bt_ps = ps.tile([P, P], BF16, name="bt_ps", tag="w", bufs=3)
+        nc.tensor.transpose(bt_ps[:], bias_rows[:], ident_b[:])
+        nc.vector.tensor_copy(out=bias_t[:], in_=bt_ps[:, 0:64])
+
+        xg = sb.tile([P, G, B, 2], F32, name="xg", align_bytes=64)
+        xt = [
+            ps.tile([P, 2, B], F32, name="xt_%d" % g, tag=("o" if g < 2 else "w"), bufs=3) for g in range(G)
+        ]
+        for bt in range(BT):
+            xw = x_sb[bt][:].bitcast(F32)
+            for g in range(G):
+                for u in range(2):
+                    nc.tensor.transpose(
+                        xt[g][:, u, P * bt : P * (bt + 1)], xw[:, 256 * g + u : 256 * (g + 1) : 2], ident_f[:]
+                    )
+        for g in range(G):
+            src = xt[g][:].rearrange("p u b -> p b u")
+            if g % 2 == 0:
+                nc.scalar.copy(out=xg[:, g], in_=src)
+            else:
+                nc.vector.tensor_copy(out=xg[:, g], in_=src)
+        nc.vector.quantize_mx(
+            out=xq[:].rearrange("p g b -> p (g b)").bitcast(FP8X4),
+            scales=xs[:].rearrange("p g b -> p (g b)"),
+            in_=xg[:].rearrange("p g b u -> p (g b u)").bitcast(BF16),
+        )
+
+        w_of_period = {1: [0, 1], 2: [2], 3: [3], 4: [4], 5: [5], 6: [6], 7: [7]}
+        for m in range(M + 1):
+            live = m < M
+            ws = w_of_period.get(m, [])
+            if live and m > 0:
+                rg(m, 0)
+            if m >= 1:
+                q(m - 1, 3)
+            if m == 1:
+                o_pass(0, 0)
+                o_pass(0, 1)
+            for wm in ws:
+                w_pass(wm, 0)
+                w_pass(wm, 1)
+            if m >= 2 and last_of[m - 2]:
+                acc_t(group_of[m - 2])
+            if m >= 2:
+                o_pass(m - 1, 0)
+                o_pass(m - 1, 1)
+            for wm in ws[:-1]:
+                evac(wm, 0)
+                evac(wm, 1)
+            if ws:
+                evac(ws[-1], 0)
+            if live:
+                rg(m, 1)
+                q(m, 0)
+            if m >= 1:
+                stt(m - 1, 0)
+            if live:
+                rg(m, 2)
+                q(m, 1)
+            if ws:
+                evac(ws[-1], 1)
+            if live:
+                rg(m, 3)
+            if m >= 1:
+                stt(m - 1, 1)
+            if live:
+                q(m, 2)
+        acc_t(group_of[M - 1])
+
+        for bt in range(BT):
+            o_sb = sb.tile([P, C], F32, name="o_sb_%d" % bt)
+            if bt == 0:
+                nc.vector.tensor_copy(out=o_sb[:], in_=acc[bt][:])
+            else:
+                nc.scalar.copy(out=o_sb[:], in_=acc[bt][:])
+            nc.sync.dma_start(out=out[P * bt : P * (bt + 1), :], in_=o_sb[:])

@@ -1,8 +1,6 @@
 from contextlib import ExitStack
 
-import concourse.bass as bass
 import concourse.mybir as mybir
-import concourse.tile as tile
 from concourse.masks import make_identity
 
 FP8X4 = mybir.dt.float8_e4m3fn_x4
@@ -22,9 +20,9 @@ CT = C // P
 BT = B // P
 FLOPS = 2 * 2 * B * D * M * C
 
-MANUAL = True
-GROUPS = [1] * 8
 RAW_BUFS = 12
+WEAVE = False
+LAST_SPLIT = 352
 
 
 def tile_multi_fuse_pic_cls_kernel(
@@ -34,8 +32,7 @@ def tile_multi_fuse_pic_cls_kernel(
     with ExitStack() as ctx:
         sb = ctx.enter_context(tc.tile_pool(name="sb", bufs=1))
         ps = ctx.enter_context(tc.psum_pool(name="ps", bufs=1))
-        if MANUAL:
-            ctx.enter_context(tc.manual_schedule())
+        ctx.enter_context(tc.manual_schedule())
 
         rs = sb.tile([P, G, M * C], U8, name="rs", align_bytes=64)
         for mp in range(4):
@@ -69,31 +66,52 @@ def tile_multi_fuse_pic_cls_kernel(
         scales_qgn = resnet_weight_scales.rearrange("g q n -> q g n")
         words_pgn = resnet_weight_words.rearrange("g p n -> p g n")
 
-        def load_rw(mp):
+        def load_sc(mp, i):
             n0 = 1024 * mp
-            for b in range(2):
-                for r in range(4):
-                    nc.sync.dma_start(
-                        out=rs[32 * b + r : P : 64, :, n0 : n0 + 1024].bitcast(I32),
-                        in_=scales_qgn[4 * b + r : 16 : 8, :, n0 : n0 + 1024].bitcast(I32),
-                    )
+            b, r = divmod(i, 4)
+            nc.sync.dma_start(
+                out=rs[32 * b + r : P : 64, :, n0 : n0 + 1024].bitcast(I32),
+                in_=scales_qgn[4 * b + r : 16 : 8, :, n0 : n0 + 1024].bitcast(I32),
+            )
+
+        def load_words(mp):
             t = sb.tile([P, G, 2048], U8, name="rwt_%d" % mp, align_bytes=64)
             nc.sync.dma_start(out=t[:].bitcast(I32), in_=words_pgn[:, :, 2048 * mp : 2048 * (mp + 1)].bitcast(I32))
             rwt.append(t)
 
         load_mw(0, 0)
+        load_mw(0, 1)
         load_x(0)
         load_x(1)
-        for g in range(1, G):
-            load_mw(0, g)
-        load_rw(0)
-        for g in range(G):
-            load_mw(1, g)
+        if WEAVE:
+            load_sc(0, 0)
+            load_sc(0, 1)
+            load_mw(0, 2)
+            load_sc(0, 2)
+            load_sc(0, 3)
+            load_mw(0, 3)
+            for i in range(4, 8):
+                load_sc(0, i)
+        else:
+            load_mw(0, 2)
+            load_mw(0, 3)
+            for i in range(8):
+                load_sc(0, i)
+        load_words(0)
         for mp in range(1, 4):
-            load_rw(mp)
-            for m in (2 * mp, 2 * mp + 1):
+            i = 0
+            for m in (2 * mp - 1, 2 * mp):
                 for g in range(G):
                     load_mw(m, g)
+                    if WEAVE:
+                        load_sc(mp, i)
+                        i += 1
+            if not WEAVE:
+                for i in range(8):
+                    load_sc(mp, i)
+            load_words(mp)
+        for g in range(G):
+            load_mw(7, g)
 
         grp = {}
         cod = {}
@@ -101,12 +119,19 @@ def tile_multi_fuse_pic_cls_kernel(
 
         def rg(m, g):
             t = sb.tile([P, C, 4], BF16, name="grp_%d_%d" % (m, g), tag="grp", bufs=4, align_bytes=64)
-            dst = t[:].rearrange("p (c i) t -> p c t i", i=4)
-            src = raw[(m, g)][:].rearrange("p t (c i) -> p c t i", i=4)
-            if g % 2 == 0:
-                nc.vector.tensor_copy(out=dst, in_=src)
-            else:
-                nc.scalar.copy(out=dst, in_=src)
+            cv = C if g % 2 == 0 else 0
+            if m == M - 1 and g == G - 1:
+                cv = LAST_SPLIT
+            if cv > 0:
+                nc.vector.tensor_copy(
+                    out=t[:, 0:cv, :].rearrange("p (c i) t -> p c t i", i=4),
+                    in_=raw[(m, g)][:, :, 0:cv].rearrange("p t (c i) -> p c t i", i=4),
+                )
+            if cv < C:
+                nc.scalar.copy(
+                    out=t[:, cv:C, :].rearrange("p (c i) t -> p c t i", i=4),
+                    in_=raw[(m, g)][:, :, cv:C].rearrange("p t (c i) -> p c t i", i=4),
+                )
             grp[(m, g)] = t
 
         def q(m, g):
@@ -124,25 +149,32 @@ def tile_multi_fuse_pic_cls_kernel(
         o_ps = {}
         w_ps = {}
         w_sb = {}
+        s_sb = {}
+
+        def bank(k, name, shape, dtype):
+            return ps.tile(shape, dtype, name=name, tag="k%d" % k)
+
+        def o_mm(dst, m, ct, g):
+            c0 = P * ct
+            nc.tensor.matmul_mx(
+                out=dst,
+                lhsT=cod[m][:, g, c0 : c0 + P].bitcast(FP8X4),
+                lhsT_scale=sca[m][:, g, c0 : c0 + P],
+                rhs=xq[:, g, :].bitcast(FP8X4),
+                rhs_scale=xs[:, g, :],
+                start=(g == 0),
+                stop=(g == G - 1),
+            )
 
         def o_pass(m, h):
-            t = ps.tile([P, 2, B], F32, name="o_%d_%d" % (m, h), tag="o", bufs=3)
+            t = bank((2 * m + h) % 3, "o_%d_%d" % (m, h), [P, 2, B], F32)
             for ctl in range(2):
-                c0 = P * (2 * h + ctl)
                 for g in range(G):
-                    nc.tensor.matmul_mx(
-                        out=t[:, ctl, :],
-                        lhsT=cod[m][:, g, c0 : c0 + P].bitcast(FP8X4),
-                        lhsT_scale=sca[m][:, g, c0 : c0 + P],
-                        rhs=xq[:, g, :].bitcast(FP8X4),
-                        rhs_scale=xs[:, g, :],
-                        start=(g == 0),
-                        stop=(g == G - 1),
-                    )
+                    o_mm(t[:, ctl, :], m, 2 * h + ctl, g)
             o_ps[(m, h)] = t
 
         def w_pass(m, h):
-            t = ps.tile([P, 2, B], F32, name="w_%d_%d" % (m, h), tag="w", bufs=3)
+            t = bank(3 + (2 * m + h) % 3, "w_%d_%d" % (m, h), [P, 2, B], F32)
             for ctl in range(2):
                 ct = 2 * h + ctl
                 n0 = C * m + P * ct
@@ -172,59 +204,46 @@ def tile_multi_fuse_pic_cls_kernel(
                 )
             w_sb[(m, h)] = t
 
-        group_of = {}
-        first_of = {}
-        last_of = {}
-        m0 = 0
-        for gi, size in enumerate(GROUPS):
-            for m in range(m0, m0 + size):
-                group_of[m] = gi
-                first_of[m] = m == m0
-                last_of[m] = m == m0 + size - 1
-            m0 += size
-        s_sb = {}
+        def stt_one(dst, src, m, ct):
+            nc.vector.scalar_tensor_tensor(
+                out=dst, in0=src, scalar=bias_t[:, CT * m + ct : CT * m + ct + 1],
+                in1=w_sb[(m, ct // 2)][:, ct % 2, :], op0=ALU.add, op1=ALU.mult,
+            )
 
         def stt(m, h):
-            gi = group_of[m]
-            if first_of[m]:
-                s_sb[(gi, h)] = sb.tile([P, 2, B], F32, name="s_%d_%d" % (gi, h), tag="s", bufs=6)
-                dst = s_sb[(gi, h)]
-            else:
-                dst = sb.tile([P, 2, B], F32, name="p_%d_%d" % (m, h), tag="p", bufs=3)
+            t = sb.tile([P, 2, B], F32, name="s_%d_%d" % (m, h), tag="s", bufs=6)
             for ctl in range(2):
-                col = CT * m + 2 * h + ctl
-                nc.vector.scalar_tensor_tensor(
-                    out=dst[:, ctl, :], in0=o_ps[(m, h)][:, ctl, :], scalar=bias_t[:, col : col + 1],
-                    in1=w_sb[(m, h)][:, ctl, :], op0=ALU.add, op1=ALU.mult,
-                )
-            if not first_of[m]:
-                nc.vector.tensor_tensor(out=s_sb[(gi, h)][:], in0=s_sb[(gi, h)][:], in1=dst[:], op=ALU.add)
+                stt_one(t[:, ctl, :], o_ps[(m, h)][:, ctl, :], m, 2 * h + ctl)
+            s_sb[(m, h)] = t
 
         acc = [ps.tile([P, C], F32, name="acc_%d" % bt) for bt in range(BT)]
 
-        def acc_t(gi):
-            for h in range(2):
-                for ctl in range(2):
-                    c0 = P * (2 * h + ctl)
-                    for bt in range(BT):
-                        nc.tensor.matmul(
-                            out=acc[bt][:, c0 : c0 + P],
-                            lhsT=s_sb[(gi, h)][:, ctl, P * bt : P * (bt + 1)],
-                            rhs=ident_f[:],
-                            start=(gi == 0 and h == 0 and ctl == 0),
-                            stop=(gi == len(GROUPS) - 1 and h == 1 and ctl == 1),
-                            is_transpose=True,
-                        )
+        def acc_one(m, ct):
+            for bt in range(BT):
+                nc.tensor.matmul(
+                    out=acc[bt][:, P * ct : P * (ct + 1)],
+                    lhsT=s_sb[(m, ct // 2)][:, ct % 2, P * bt : P * (bt + 1)],
+                    rhs=ident_f[:],
+                    start=(m == 0 and ct == 0),
+                    stop=(m == M - 1 and ct == CT - 1),
+                    is_transpose=True,
+                )
+
+        def acc_t(m):
+            for ct in range(CT):
+                acc_one(m, ct)
 
         rg(0, 0)
-        bt_ps = ps.tile([P, P], BF16, name="bt_ps", tag="w", bufs=3)
+        rg(0, 1)
+        bt_ps = bank(5, "bt_ps", [P, P], BF16)
         nc.tensor.transpose(bt_ps[:], bias_rows[:], ident_b[:])
         nc.vector.tensor_copy(out=bias_t[:], in_=bt_ps[:, 0:64])
+        q(0, 0)
+        q(0, 1)
+        rg(0, 2)
 
         xg = sb.tile([P, G, B, 2], F32, name="xg", align_bytes=64)
-        xt = [
-            ps.tile([P, 2, B], F32, name="xt_%d" % g, tag=("o" if g < 2 else "w"), bufs=3) for g in range(G)
-        ]
+        xt = [bank(g, "xt_%d" % g, [P, 2, B], F32) for g in range(G)]
         for bt in range(BT):
             xw = x_sb[bt][:].bitcast(F32)
             for g in range(G):
@@ -243,48 +262,58 @@ def tile_multi_fuse_pic_cls_kernel(
             scales=xs[:].rearrange("p g b -> p (g b)"),
             in_=xg[:].rearrange("p g b u -> p (g b u)").bitcast(BF16),
         )
+        rg(0, 3)
+        q(0, 2)
+        w_pass(0, 0)
+        w_pass(0, 1)
 
-        w_of_period = {1: [0, 1], 2: [2], 3: [3], 4: [4], 5: [5], 6: [6], 7: [7]}
-        for m in range(M + 1):
-            live = m < M
-            ws = w_of_period.get(m, [])
-            if live and m > 0:
-                rg(m, 0)
-            if m >= 1:
-                q(m - 1, 3)
-            if m == 1:
-                o_pass(0, 0)
-                o_pass(0, 1)
-            for wm in ws:
-                w_pass(wm, 0)
-                w_pass(wm, 1)
-            if m >= 2 and last_of[m - 2]:
-                acc_t(group_of[m - 2])
-            if m >= 2:
-                o_pass(m - 1, 0)
-                o_pass(m - 1, 1)
-            for wm in ws[:-1]:
-                evac(wm, 0)
-                evac(wm, 1)
-            if ws:
-                evac(ws[-1], 0)
-            if live:
-                rg(m, 1)
-                q(m, 0)
-            if m >= 1:
-                stt(m - 1, 0)
-            if live:
-                rg(m, 2)
+        for m in range(1, M):
+            rg(m, 0)
+            q(m - 1, 3)
+            o_pass(m - 1, 0)
+            o_pass(m - 1, 1)
+            evac(m - 1, 0)
+            rg(m, 1)
+            rg(m, 2)
+            q(m, 0)
+            if m < M - 1:
                 q(m, 1)
-            if ws:
-                evac(ws[-1], 1)
-            if live:
+                stt(m - 1, 0)
+                evac(m - 1, 1)
                 rg(m, 3)
-            if m >= 1:
-                stt(m - 1, 1)
-            if live:
                 q(m, 2)
-        acc_t(group_of[M - 1])
+                stt(m - 1, 1)
+                w_pass(m, 0)
+                w_pass(m, 1)
+                if m == M - 2:
+                    w_pass(M - 1, 0)
+                acc_t(m - 1)
+                if m == M - 2:
+                    w_pass(M - 1, 1)
+
+        m = M - 1
+        stt(m - 1, 0)
+        q(m, 1)
+        evac(m - 1, 1)
+        stt(m - 1, 1)
+        evac(m, 0)
+        evac(m, 1)
+        rg(m, 3)
+        q(m, 2)
+        acc_t(m - 1)
+        last_banks = [2, 0, 1, 4]
+        o_last = [bank(last_banks[ct], "o_last_%d" % ct, [P, B], F32) for ct in range(CT)]
+        for g in range(G - 1):
+            for ct in range(CT):
+                o_mm(o_last[ct][:], m, ct, g)
+        q(m, 3)
+        for h in range(2):
+            s_sb[(m, h)] = sb.tile([P, 2, B], F32, name="s_%d_%d" % (m, h), tag="s", bufs=6)
+        for ct in range(CT):
+            o_mm(o_last[ct][:], m, ct, G - 1)
+        for ct in range(CT):
+            stt_one(s_sb[(m, ct // 2)][:, ct % 2, :], o_last[ct][:], m, ct)
+            acc_one(m, ct)
 
         for bt in range(BT):
             o_sb = sb.tile([P, C], F32, name="o_sb_%d" % bt)

@@ -21,7 +21,7 @@ BT = B // P
 FLOPS = 2 * 2 * B * D * M * C
 
 RAW_BUFS = 12
-WEAVE = False
+WEAVE = True
 LAST_SPLIT = 352
 
 

@@ -21,7 +21,8 @@ BT = B // P
 FLOPS = 2 * 2 * B * D * M * C
 
 RAW_BUFS = 12
-WEAVE = True
+WORDS_AFTER = {1: 11, 2: 19, 3: 23}
+W_OF_PERIOD = {0: [0], 1: [1], 2: [2], 3: [3], 4: [4], 5: [5, 6], 6: [7]}
 LAST_SPLIT = 352
 
 
@@ -34,11 +35,11 @@ def tile_multi_fuse_pic_cls_kernel(
         ps = ctx.enter_context(tc.psum_pool(name="ps", bufs=1))
         ctx.enter_context(tc.manual_schedule())
 
+        bias_rows = sb.tile([P, P], BF16, name="bias_rows")
+        nc.vector.memset(bias_rows[:], 0.0)
         rs = sb.tile([P, G, M * C], U8, name="rs", align_bytes=64)
         for mp in range(4):
             nc.vector.memset(rs[:, :, 1024 * mp : 1024 * (mp + 1)].bitcast(I32), 0)
-        bias_rows = sb.tile([P, P], BF16, name="bias_rows")
-        nc.vector.memset(bias_rows[:], 0.0)
         ident_f = sb.tile([P, P], F32, name="ident_f")
         make_identity(nc, ident_f[:])
         ident_b = sb.tile([P, P], BF16, name="ident_b")
@@ -80,38 +81,29 @@ def tile_multi_fuse_pic_cls_kernel(
             rwt.append(t)
 
         load_mw(0, 0)
-        load_mw(0, 1)
         load_x(0)
         load_x(1)
-        if WEAVE:
-            load_sc(0, 0)
-            load_sc(0, 1)
-            load_mw(0, 2)
-            load_sc(0, 2)
-            load_sc(0, 3)
-            load_mw(0, 3)
-            for i in range(4, 8):
-                load_sc(0, i)
-        else:
-            load_mw(0, 2)
-            load_mw(0, 3)
-            for i in range(8):
-                load_sc(0, i)
+        load_sc(0, 0)
+        load_sc(0, 1)
+        for g in range(1, G):
+            load_mw(0, g)
+            load_sc(0, 2 * g)
+            load_sc(0, 2 * g + 1)
         load_words(0)
+        first = 4
         for mp in range(1, 4):
+            last = WORDS_AFTER[mp]
+            per = 8 // (last - first + 1)
             i = 0
-            for m in (2 * mp - 1, 2 * mp):
-                for g in range(G):
-                    load_mw(m, g)
-                    if WEAVE:
-                        load_sc(mp, i)
-                        i += 1
-            if not WEAVE:
-                for i in range(8):
+            for c in range(first, last + 1):
+                load_mw(c // 4, c % 4)
+                for k in range(per):
                     load_sc(mp, i)
+                    i += 1
             load_words(mp)
-        for g in range(G):
-            load_mw(7, g)
+            first = last + 1
+        for c in range(first, 4 * M):
+            load_mw(c // 4, c % 4)
 
         grp = {}
         cod = {}
@@ -234,14 +226,6 @@ def tile_multi_fuse_pic_cls_kernel(
                 acc_one(m, ct)
 
         rg(0, 0)
-        rg(0, 1)
-        bt_ps = bank(5, "bt_ps", [P, P], BF16)
-        nc.tensor.transpose(bt_ps[:], bias_rows[:], ident_b[:])
-        nc.vector.tensor_copy(out=bias_t[:], in_=bt_ps[:, 0:64])
-        q(0, 0)
-        q(0, 1)
-        rg(0, 2)
-
         xg = sb.tile([P, G, B, 2], F32, name="xg", align_bytes=64)
         xt = [bank(g, "xt_%d" % g, [P, 2, B], F32) for g in range(G)]
         for bt in range(BT):
@@ -262,10 +246,18 @@ def tile_multi_fuse_pic_cls_kernel(
             scales=xs[:].rearrange("p g b -> p (g b)"),
             in_=xg[:].rearrange("p g b u -> p (g b u)").bitcast(BF16),
         )
+        bt_ps = bank(5, "bt_ps", [P, P], BF16)
+        nc.tensor.transpose(bt_ps[:], bias_rows[:], ident_b[:])
+        nc.vector.tensor_copy(out=bias_t[:], in_=bt_ps[:, 0:64])
+        q(0, 0)
+        rg(0, 1)
+        rg(0, 2)
+        q(0, 1)
         rg(0, 3)
         q(0, 2)
-        w_pass(0, 0)
-        w_pass(0, 1)
+        for wm in W_OF_PERIOD[0]:
+            w_pass(wm, 0)
+            w_pass(wm, 1)
 
         for m in range(1, M):
             rg(m, 0)
@@ -283,29 +275,28 @@ def tile_multi_fuse_pic_cls_kernel(
                 rg(m, 3)
                 q(m, 2)
                 stt(m - 1, 1)
-                w_pass(m, 0)
-                w_pass(m, 1)
-                if m == M - 2:
-                    w_pass(M - 1, 0)
+                for wm in W_OF_PERIOD[m]:
+                    w_pass(wm, 0)
+                    w_pass(wm, 1)
                 acc_t(m - 1)
-                if m == M - 2:
-                    w_pass(M - 1, 1)
 
         m = M - 1
-        stt(m - 1, 0)
-        q(m, 1)
         evac(m - 1, 1)
-        stt(m - 1, 1)
         evac(m, 0)
-        evac(m, 1)
-        rg(m, 3)
-        q(m, 2)
-        acc_t(m - 1)
-        last_banks = [2, 0, 1, 4]
+        q(m, 1)
+        stt(m - 1, 0)
+        last_banks = [2, 4, 5, 0]
         o_last = [bank(last_banks[ct], "o_last_%d" % ct, [P, B], F32) for ct in range(CT)]
-        for g in range(G - 1):
+        for g in range(2):
             for ct in range(CT):
                 o_mm(o_last[ct][:], m, ct, g)
+        rg(m, 3)
+        stt(m - 1, 1)
+        evac(m, 1)
+        q(m, 2)
+        acc_t(m - 1)
+        for ct in range(CT):
+            o_mm(o_last[ct][:], m, ct, 2)
         q(m, 3)
         for h in range(2):
             s_sb[(m, h)] = sb.tile([P, 2, B], F32, name="s_%d_%d" % (m, h), tag="s", bufs=6)

@@ -35,11 +35,10 @@ def tile_multi_fuse_pic_cls_kernel(
         ps = ctx.enter_context(tc.psum_pool(name="ps", bufs=1))
         ctx.enter_context(tc.manual_schedule())
 
+        rs = sb.tile([P, G, M * C], U8, name="rs", align_bytes=64)
+        nc.vector.memset(rs[:].bitcast(I32), 0)
         bias_rows = sb.tile([P, P], BF16, name="bias_rows")
         nc.vector.memset(bias_rows[:], 0.0)
-        rs = sb.tile([P, G, M * C], U8, name="rs", align_bytes=64)
-        for mp in range(4):
-            nc.vector.memset(rs[:, :, 1024 * mp : 1024 * (mp + 1)].bitcast(I32), 0)
         ident_f = sb.tile([P, P], F32, name="ident_f")
         make_identity(nc, ident_f[:])
         ident_b = sb.tile([P, P], BF16, name="ident_b")
@@ -67,12 +66,11 @@ def tile_multi_fuse_pic_cls_kernel(
         scales_qgn = resnet_weight_scales.rearrange("g q n -> q g n")
         words_pgn = resnet_weight_words.rearrange("g p n -> p g n")
 
-        def load_sc(mp, i):
-            n0 = 1024 * mp
+        for i in range(8):
             b, r = divmod(i, 4)
-            nc.sync.dma_start(
-                out=rs[32 * b + r : P : 64, :, n0 : n0 + 1024].bitcast(I32),
-                in_=scales_qgn[4 * b + r : 16 : 8, :, n0 : n0 + 1024].bitcast(I32),
+            nc.gpsimd.dma_start(
+                out=rs[32 * b + r : P : 64, :, :].bitcast(F32),
+                in_=scales_qgn[4 * b + r : 16 : 8, :, :].bitcast(F32),
             )
 
         def load_words(mp):
@@ -83,23 +81,14 @@ def tile_multi_fuse_pic_cls_kernel(
         load_mw(0, 0)
         load_x(0)
         load_x(1)
-        load_sc(0, 0)
-        load_sc(0, 1)
         for g in range(1, G):
             load_mw(0, g)
-            load_sc(0, 2 * g)
-            load_sc(0, 2 * g + 1)
         load_words(0)
         first = 4
         for mp in range(1, 4):
             last = WORDS_AFTER[mp]
-            per = 8 // (last - first + 1)
-            i = 0
             for c in range(first, last + 1):
                 load_mw(c // 4, c % 4)
-                for k in range(per):
-                    load_sc(mp, i)
-                    i += 1
             load_words(mp)
             first = last + 1
         for c in range(first, 4 * M):

@@ -21,8 +21,7 @@ BT = B // P
 FLOPS = 2 * 2 * B * D * M * C
 
 RAW_BUFS = 12
-WORDS_AFTER = {1: 11, 2: 19, 3: 23}
-W_OF_PERIOD = {0: [0], 1: [1], 2: [2], 3: [3], 4: [4], 5: [5, 6], 6: [7]}
+WORDS_AFTER = {1: 7, 2: 15, 3: 23}
 LAST_SPLIT = 352
 
 
@@ -35,10 +34,11 @@ def tile_multi_fuse_pic_cls_kernel(
         ps = ctx.enter_context(tc.psum_pool(name="ps", bufs=1))
         ctx.enter_context(tc.manual_schedule())
 
-        rs = sb.tile([P, G, M * C], U8, name="rs", align_bytes=64)
-        nc.vector.memset(rs[:].bitcast(I32), 0)
         bias_rows = sb.tile([P, P], BF16, name="bias_rows")
         nc.vector.memset(bias_rows[:], 0.0)
+        rs = sb.tile([P, G, M * C], U8, name="rs", align_bytes=64)
+        for mp in range(4):
+            nc.vector.memset(rs[:, :, 1024 * mp : 1024 * (mp + 1)].bitcast(I32), 0)
         ident_f = sb.tile([P, P], F32, name="ident_f")
         make_identity(nc, ident_f[:])
         ident_b = sb.tile([P, P], BF16, name="ident_b")
@@ -66,11 +66,12 @@ def tile_multi_fuse_pic_cls_kernel(
         scales_qgn = resnet_weight_scales.rearrange("g q n -> q g n")
         words_pgn = resnet_weight_words.rearrange("g p n -> p g n")
 
-        for i in range(8):
+        def load_sc(mp, i):
+            n0 = 1024 * mp
             b, r = divmod(i, 4)
-            nc.gpsimd.dma_start(
-                out=rs[32 * b + r : P : 64, :, :].bitcast(F32),
-                in_=scales_qgn[4 * b + r : 16 : 8, :, :].bitcast(F32),
+            nc.sync.dma_start(
+                out=rs[32 * b + r : P : 64, :, n0 : n0 + 1024].bitcast(I32),
+                in_=scales_qgn[4 * b + r : 16 : 8, :, n0 : n0 + 1024].bitcast(I32),
             )
 
         def load_words(mp):
@@ -81,14 +82,23 @@ def tile_multi_fuse_pic_cls_kernel(
         load_mw(0, 0)
         load_x(0)
         load_x(1)
+        for i in range(4):
+            load_sc(0, i)
+        load_words(0)
+        for i in range(4, 8):
+            load_sc(0, i)
         for g in range(1, G):
             load_mw(0, g)
-        load_words(0)
         first = 4
         for mp in range(1, 4):
             last = WORDS_AFTER[mp]
+            per = 8 // (last - first + 1)
+            i = 0
             for c in range(first, last + 1):
                 load_mw(c // 4, c % 4)
+                for k in range(per):
+                    load_sc(mp, i)
+                    i += 1
             load_words(mp)
             first = last + 1
         for c in range(first, 4 * M):
@@ -238,40 +248,40 @@ def tile_multi_fuse_pic_cls_kernel(
         bt_ps = bank(5, "bt_ps", [P, P], BF16)
         nc.tensor.transpose(bt_ps[:], bias_rows[:], ident_b[:])
         nc.vector.tensor_copy(out=bias_t[:], in_=bt_ps[:, 0:64])
-        q(0, 0)
-        rg(0, 1)
-        rg(0, 2)
-        q(0, 1)
-        rg(0, 3)
-        q(0, 2)
-        for wm in W_OF_PERIOD[0]:
+        for wm in (0, 1):
             w_pass(wm, 0)
             w_pass(wm, 1)
+        q(0, 0)
+        rg(0, 1)
+        evac(0, 0)
+        rg(0, 2)
+        q(0, 1)
+        evac(0, 1)
+        rg(0, 3)
+        q(0, 2)
 
         for m in range(1, M):
             rg(m, 0)
             q(m - 1, 3)
             o_pass(m - 1, 0)
             o_pass(m - 1, 1)
-            evac(m - 1, 0)
+            evac(m, 0)
             rg(m, 1)
             rg(m, 2)
             q(m, 0)
             if m < M - 1:
                 q(m, 1)
                 stt(m - 1, 0)
-                evac(m - 1, 1)
+                evac(m, 1)
                 rg(m, 3)
                 q(m, 2)
                 stt(m - 1, 1)
-                for wm in W_OF_PERIOD[m]:
-                    w_pass(wm, 0)
-                    w_pass(wm, 1)
+                w_pass(m + 1, 0)
+                w_pass(m + 1, 1)
                 acc_t(m - 1)
 
         m = M - 1
-        evac(m - 1, 1)
-        evac(m, 0)
+        evac(m, 1)
         q(m, 1)
         stt(m - 1, 0)
         last_banks = [2, 4, 5, 0]
@@ -281,7 +291,6 @@ def tile_multi_fuse_pic_cls_kernel(
                 o_mm(o_last[ct][:], m, ct, g)
         rg(m, 3)
         stt(m - 1, 1)
-        evac(m, 1)
         q(m, 2)
         acc_t(m - 1)
         for ct in range(CT):

from contextlib import ExitStack

import concourse.mybir as mybir
from concourse.masks import make_identity

FP8X4 = mybir.dt.float8_e4m3fn_x4
FP4X4 = mybir.dt.float4_e2m1fn_x4
BF16 = mybir.dt.bfloat16
F32 = mybir.dt.float32
I32 = mybir.dt.int32
U32 = mybir.dt.uint32
U8 = mybir.dt.uint8
ACT = mybir.ActivationFunctionType
ALU = mybir.AluOpType

B, D, M, C = 256, 2048, 8, 512
P = 128
G = D // 512
CT = C // P
BT = B // P
FLOPS = 2 * 2 * B * D * M * C

RAW_BUFS = 12
WORDS_AFTER = {1: 7, 2: 15, 3: 23}
LAST_SPLIT = 352


def tile_multi_fuse_pic_cls_kernel(
    tc, x, model_weights, model_bias, resnet_weight_words, resnet_weight_scales, resnet_bias, out
):
    nc = tc.nc
    with ExitStack() as ctx:
        sb = ctx.enter_context(tc.tile_pool(name="sb", bufs=1))
        ps = ctx.enter_context(tc.psum_pool(name="ps", bufs=1))
        ctx.enter_context(tc.manual_schedule())

        bias_rows = sb.tile([P, P], BF16, name="bias_rows")
        nc.vector.memset(bias_rows[:], 0.0)
        rs = sb.tile([P, G, M * C], U8, name="rs", align_bytes=64)
        for mp in range(4):
            nc.vector.memset(rs[:, :, 1024 * mp : 1024 * (mp + 1)].bitcast(I32), 0)
        ident_f = sb.tile([P, P], F32, name="ident_f")
        make_identity(nc, ident_f[:])
        ident_b = sb.tile([P, P], BF16, name="ident_b")
        make_identity(nc, ident_b[:])

        nc.scalar.dma_start(out=bias_rows[0:32, :], in_=model_bias.rearrange("m (t c) -> (m t) c", c=P))
        nc.scalar.dma_start(out=bias_rows[32:64, :], in_=resnet_bias.rearrange("(r c) -> r c", c=P))

        raw = {}
        x_sb = []
        rwt = []

        def load_mw(m, g):
            t = sb.tile([P, 4, C], BF16, name="raw_%d_%d" % (m, g), tag="raw", bufs=RAW_BUFS)
            nc.sync.dma_start(
                out=t[:], in_=model_weights[m, 512 * g : 512 * (g + 1), :].rearrange("(p j) c -> p j c", j=4)
            )
            raw[(m, g)] = t

        def load_x(bt):
            t = sb.tile([P, D], BF16, name="x_sb_%d" % bt)
            nc.sync.dma_start(out=t[:], in_=x[P * bt : P * (bt + 1), :])
            x_sb.append(t)

        scales_qgn = resnet_weight_scales.rearrange("g q n -> q g n")
        words_pgn = resnet_weight_words.rearrange("g p n -> p g n")

        def load_sc(mp, i):
            n0 = 1024 * mp
            b, r = divmod(i, 4)
            nc.sync.dma_start(
                out=rs[32 * b + r : P : 64, :, n0 : n0 + 1024].bitcast(I32),
                in_=scales_qgn[4 * b + r : 16 : 8, :, n0 : n0 + 1024].bitcast(I32),
            )

        def load_words(mp):
            t = sb.tile([P, G, 2048], U8, name="rwt_%d" % mp, align_bytes=64)
            nc.sync.dma_start(out=t[:].bitcast(I32), in_=words_pgn[:, :, 2048 * mp : 2048 * (mp + 1)].bitcast(I32))
            rwt.append(t)

        load_mw(0, 0)
        load_x(0)
        load_x(1)
        for i in range(4):
            load_sc(0, i)
        load_words(0)
        for i in range(4, 8):
            load_sc(0, i)
        for g in range(1, G):
            load_mw(0, g)
        first = 4
        for mp in range(1, 4):
            last = WORDS_AFTER[mp]
            per = 8 // (last - first + 1)
            i = 0
            for c in range(first, last + 1):
                load_mw(c // 4, c % 4)
                for k in range(per):
                    load_sc(mp, i)
                    i += 1
            load_words(mp)
            first = last + 1
        for c in range(first, 4 * M):
            load_mw(c // 4, c % 4)

        grp = {}
        cod = {}
        sca = {}

        def rg(m, g):
            t = sb.tile([P, C, 4], BF16, name="grp_%d_%d" % (m, g), tag="grp", bufs=4, align_bytes=64)
            cv = C if g % 2 == 0 else 0
            if m == M - 1 and g == G - 1:
                cv = LAST_SPLIT
            if cv > 0:
                nc.vector.tensor_copy(
                    out=t[:, 0:cv, :].rearrange("p (c i) t -> p c t i", i=4),
                    in_=raw[(m, g)][:, :, 0:cv].rearrange("p t (c i) -> p c t i", i=4),
                )
            if cv < C:
                nc.scalar.copy(
                    out=t[:, cv:C, :].rearrange("p (c i) t -> p c t i", i=4),
                    in_=raw[(m, g)][:, :, cv:C].rearrange("p t (c i) -> p c t i", i=4),
                )
            grp[(m, g)] = t

        def q(m, g):
            if g == 0:
                cod[m] = sb.tile([P, G, C], U32, name="cod_%d" % m, tag="cod", bufs=3, align_bytes=64)
                sca[m] = sb.tile([P, G, C], U8, name="sca_%d" % m, tag="sca", bufs=3, align_bytes=64)
            nc.vector.quantize_mx(
                out=cod[m][:, g, :].bitcast(FP8X4),
                scales=sca[m][:, g, :],
                in_=grp[(m, g)][:].rearrange("p c t -> p (c t)"),
            )

        xq = sb.tile([P, G, B], U32, name="xq", align_bytes=64)
        xs = sb.tile([P, G, B], U8, name="xs", align_bytes=64)
        o_ps = {}
        w_ps = {}
        w_sb = {}
        s_sb = {}

        def bank(k, name, shape, dtype):
            return ps.tile(shape, dtype, name=name, tag="k%d" % k)

        def o_mm(dst, m, ct, g):
            c0 = P * ct
            nc.tensor.matmul_mx(
                out=dst,
                lhsT=cod[m][:, g, c0 : c0 + P].bitcast(FP8X4),
                lhsT_scale=sca[m][:, g, c0 : c0 + P],
                rhs=xq[:, g, :].bitcast(FP8X4),
                rhs_scale=xs[:, g, :],
                start=(g == 0),
                stop=(g == G - 1),
            )

        def o_pass(m, h):
            t = bank((2 * m + h) % 3, "o_%d_%d" % (m, h), [P, 2, B], F32)
            for ctl in range(2):
                for g in range(G):
                    o_mm(t[:, ctl, :], m, 2 * h + ctl, g)
            o_ps[(m, h)] = t

        def w_pass(m, h):
            t = bank(3 + (2 * m + h) % 3, "w_%d_%d" % (m, h), [P, 2, B], F32)
            for ctl in range(2):
                ct = 2 * h + ctl
                n0 = C * m + P * ct
                w0 = 2 * (C * (m % 2) + P * ct)
                for bt in range(BT):
                    for g in range(G):
                        nc.tensor.matmul_mx(
                            out=t[:, ctl, P * bt : P * (bt + 1)],
                            lhsT=rwt[m // 2][:, g, w0 : w0 + 2 * P].bitcast(FP4X4),
                            lhsT_scale=rs[:, g, n0 : n0 + P],
                            rhs=xq[:, g, P * bt : P * (bt + 1)].bitcast(FP8X4),
                            rhs_scale=xs[:, g, P * bt : P * (bt + 1)],
                            start=(g == 0),
                            stop=(g == G - 1),
                        )
            w_ps[(m, h)] = t

        bias_t = sb.tile([P, 64], F32, name="bias_t")

        def evac(m, h):
            t = sb.tile([P, 2, B], F32, name="wsb_%d_%d" % (m, h), tag="wsb", bufs=6)
            for ctl in range(2):
                col = 32 + CT * m + 2 * h + ctl
                nc.scalar.activation(
                    out=t[:, ctl, :], in_=w_ps[(m, h)][:, ctl, :], func=ACT.Identity,
                    bias=bias_t[:, col : col + 1], scale=1.0,
                )
            w_sb[(m, h)] = t

        def stt_one(dst, src, m, ct):
            nc.vector.scalar_tensor_tensor(
                out=dst, in0=src, scalar=bias_t[:, CT * m + ct : CT * m + ct + 1],
                in1=w_sb[(m, ct // 2)][:, ct % 2, :], op0=ALU.add, op1=ALU.mult,
            )

        def stt(m, h):
            t = sb.tile([P, 2, B], F32, name="s_%d_%d" % (m, h), tag="s", bufs=6)
            for ctl in range(2):
                stt_one(t[:, ctl, :], o_ps[(m, h)][:, ctl, :], m, 2 * h + ctl)
            s_sb[(m, h)] = t

        acc = [ps.tile([P, C], F32, name="acc_%d" % bt) for bt in range(BT)]

        def acc_one(m, ct):
            for bt in range(BT):
                nc.tensor.matmul(
                    out=acc[bt][:, P * ct : P * (ct + 1)],
                    lhsT=s_sb[(m, ct // 2)][:, ct % 2, P * bt : P * (bt + 1)],
                    rhs=ident_f[:],
                    start=(m == 0 and ct == 0),
                    stop=(m == M - 1 and ct == CT - 1),
                    is_transpose=True,
                )

        def acc_t(m):
            for ct in range(CT):
                acc_one(m, ct)

        rg(0, 0)
        xg = sb.tile([P, G, B, 2], F32, name="xg", align_bytes=64)
        xt = [bank(g, "xt_%d" % g, [P, 2, B], F32) for g in range(G)]
        for bt in range(BT):
            xw = x_sb[bt][:].bitcast(F32)
            for g in range(G):
                for u in range(2):
                    nc.tensor.transpose(
                        xt[g][:, u, P * bt : P * (bt + 1)], xw[:, 256 * g + u : 256 * (g + 1) : 2], ident_f[:]
                    )
        for g in range(G):
            src = xt[g][:].rearrange("p u b -> p b u")
            if g % 2 == 0:
                nc.scalar.copy(out=xg[:, g], in_=src)
            else:
                nc.vector.tensor_copy(out=xg[:, g], in_=src)
        nc.vector.quantize_mx(
            out=xq[:].rearrange("p g b -> p (g b)").bitcast(FP8X4),
            scales=xs[:].rearrange("p g b -> p (g b)"),
            in_=xg[:].rearrange("p g b u -> p (g b u)").bitcast(BF16),
        )
        bt_ps = bank(5, "bt_ps", [P, P], BF16)
        nc.tensor.transpose(bt_ps[:], bias_rows[:], ident_b[:])
        nc.vector.tensor_copy(out=bias_t[:], in_=bt_ps[:, 0:64])
        for wm in (0, 1):
            w_pass(wm, 0)
            w_pass(wm, 1)
        q(0, 0)
        rg(0, 1)
        evac(0, 0)
        rg(0, 2)
        q(0, 1)
        evac(0, 1)
        rg(0, 3)
        q(0, 2)

        for m in range(1, M):
            rg(m, 0)
            q(m - 1, 3)
            o_pass(m - 1, 0)
            o_pass(m - 1, 1)
            evac(m, 0)
            rg(m, 1)
            rg(m, 2)
            q(m, 0)
            if m < M - 1:
                q(m, 1)
                stt(m - 1, 0)
                evac(m, 1)
                rg(m, 3)
                q(m, 2)
                stt(m - 1, 1)
                w_pass(m + 1, 0)
                w_pass(m + 1, 1)
                acc_t(m - 1)

        m = M - 1
        evac(m, 1)
        q(m, 1)
        stt(m - 1, 0)
        last_banks = [2, 4, 5, 0]
        o_last = [bank(last_banks[ct], "o_last_%d" % ct, [P, B], F32) for ct in range(CT)]
        for g in range(2):
            for ct in range(CT):
                o_mm(o_last[ct][:], m, ct, g)
        rg(m, 3)
        stt(m - 1, 1)
        q(m, 2)
        acc_t(m - 1)
        for ct in range(CT):
            o_mm(o_last[ct][:], m, ct, 2)
        q(m, 3)
        for h in range(2):
            s_sb[(m, h)] = sb.tile([P, 2, B], F32, name="s_%d_%d" % (m, h), tag="s", bufs=6)
        for ct in range(CT):
            o_mm(o_last[ct][:], m, ct, G - 1)
        for ct in range(CT):
            stt_one(s_sb[(m, ct // 2)][:, ct % 2, :], o_last[ct][:], m, ct)
            acc_one(m, ct)

        for bt in range(BT):
            o_sb = sb.tile([P, C], F32, name="o_sb_%d" % bt)
            if bt == 0:
                nc.vector.tensor_copy(out=o_sb[:], in_=acc[bt][:])
            else:
                nc.scalar.copy(out=o_sb[:], in_=acc[bt][:])
            nc.sync.dma_start(out=out[P * bt : P * (bt + 1), :], in_=o_sb[:])
